import numpy as np
import ml_dtypes


def mxq(x, axis, fmt="e4m3"):
    dtype, down = {"e4m3": (ml_dtypes.float8_e4m3fn, 7), "e5m2": (ml_dtypes.float8_e5m2, 14)}[fmt]
    v = np.moveaxis(np.asarray(x, np.float32).astype(ml_dtypes.bfloat16).astype(np.float64), axis, -1)
    blocks = v.reshape(v.shape[:-1] + (-1, 32))
    amax = np.abs(blocks).max(-1, keepdims=True)
    byte = np.maximum(np.where(amax > 0, np.frexp(amax)[1] - 1 + 127, 0) - down, 1)
    scale = np.exp2(byte - 127.0)
    codes = (blocks / scale).astype(np.float32).astype(dtype).astype(np.float64)
    return np.moveaxis((codes * scale).reshape(v.shape), -1, axis)


WIDE = False


def mx_kscale(k):
    if not WIDE:
        return np.ones(k)
    levels = np.array([10, -10, 5, -5, 0])
    if k % 512:
        return np.exp2(np.random.permutation(np.resize(levels, k // 32))).repeat(32)
    a = np.empty((k // 512, 16))
    for p in range(k // 512):
        a[p, :8] = np.random.permutation(np.resize(levels, 8))
        for g in range(8):
            far = levels[np.abs(levels - a[p, g]) >= 10]
            a[p, g + 8] = far[np.random.randint(len(far))]
    return np.exp2(a.ravel()).repeat(32)


BF16 = ml_dtypes.bfloat16


def bf(x):
    return np.asarray(x, np.float32).astype(BF16)


def f64(x):
    return np.asarray(x).astype(np.float64)


B, C, HH, WW = 1, 512, 32, 32
N = HH * WW


def setup_inputs():
    s, t = mx_kscale(N), mx_kscale(C)
    z = np.random.standard_normal((B, N, N)) * 2.0
    e = np.exp(z - z.max(-1, keepdims=True))
    return {"attention": bf(e / e.sum(-1, keepdims=True) * s[None, None, :]),
            "v": bf(np.random.standard_normal((B, N, C)) * 2.0 / s[None, :, None] * t[None, None, :]),
            "x": bf(np.random.standard_normal((B, C, HH, WW))),
            "Wo": bf(np.random.standard_normal((C, C)) * 2.0 / np.sqrt(C) / t[None, :]),
            "bo": bf(np.random.standard_normal(C) * 0.2)}


def reference(attention, v, x, Wo, bo):
    h = mxq(f64(attention), 2, "e4m3") @ mxq(f64(v), 1, "e4m3")
    out = mxq(f64(Wo), 1, "e4m3") @ mxq(h, 2, "e4m3").transpose(0, 2, 1)
    out = out.reshape(B, C, HH, WW) + f64(bo)[None, :, None, None]
    return f64(x) + out

@@ -1,0 +1,234 @@
+from contextlib import ExitStack
+
+import concourse.mybir as mybir
+from concourse.masks import make_identity
+
+F32 = mybir.dt.float32
+BF16 = mybir.dt.bfloat16
+U32 = mybir.dt.uint32
+U8 = mybir.dt.uint8
+FP8X4 = mybir.dt.float8_e4m3fn_x4
+ADD = mybir.AluOpType.add
+
+P = 128
+PACK = 4
+K_PASS = P * PACK
+
+TOKENS = 1024
+CHANNELS = 512
+M_PASSES = TOKENS // K_PASS
+C_TILES = CHANNELS // P
+O_TILES = CHANNELS // P
+BLOCKS = TOKENS // P
+CHUNK_BLOCKS = 2
+CHUNK = CHUNK_BLOCKS * P
+CHUNKS = BLOCKS // CHUNK_BLOCKS
+BANK_F32 = 512
+O_TILES_PER_BANK = BANK_F32 // CHUNK
+
+FLOPS = 2 * TOKENS * TOKENS * CHANNELS + 2 * CHANNELS * CHANNELS * TOKENS
+
+
+def tile_visionattention_pb_kernel(tc, attention, v, x, Wo, bo, out):
+    nc = tc.nc
+
+    attention_blocks = attention.rearrange("b (k p) m -> (b k) p m", p=P)
+    v_passes = v.rearrange("b (g q j) c -> (b g) q j c", g=M_PASSES, j=PACK)
+    wo_tiles = Wo.rearrange("(t p) c -> p t c", p=P)
+    bo_rows_dram = bo.rearrange("(t p) -> t p", p=P)
+    x_tiles = x.rearrange("b (t p) i j -> p (b t) (i j)", p=P)
+    y_tiles = out.rearrange("b (t p) i j -> p (b t) (i j)", p=P)
+
+    with ExitStack() as ctx:
+        keep = ctx.enter_context(tc.tile_pool(name="keep", bufs=1))
+        a_pool = ctx.enter_context(tc.tile_pool(name="a", bufs=BLOCKS))
+        h_pool = ctx.enter_context(tc.tile_pool(name="h", bufs=2))
+        y_pool = ctx.enter_context(tc.tile_pool(name="y", bufs=2 * O_TILES))
+        psum_t = ctx.enter_context(tc.psum_pool(name="psum_t", bufs=4))
+        psum_h = ctx.enter_context(tc.psum_pool(name="psum_h", bufs=2))
+        psum_p = ctx.enter_context(tc.psum_pool(name="psum_p", bufs=2))
+
+        identity_f32 = keep.tile([P, P], F32)
+        make_identity(nc, identity_f32[:])
+        identity_bf16 = keep.tile([P, P], BF16)
+        make_identity(nc, identity_bf16[:])
+
+        v_raw = keep.tile([P, M_PASSES, PACK, CHANNELS], BF16)
+        wo_raw = keep.tile([P, O_TILES, CHANNELS], BF16)
+        x_sb = keep.tile([P, O_TILES, TOKENS], BF16)
+        a_raw = {}
+
+        def load_attention(k):
+            for b in range(k * CHUNK_BLOCKS, (k + 1) * CHUNK_BLOCKS):
+                raw = a_pool.tile([P, TOKENS], BF16, tag="a_raw")
+                nc.sync.dma_start(out=raw[:], in_=attention_blocks[b])
+                a_raw[b] = raw
+
+        def load_x_half(half):
+            cols = slice(half * TOKENS // 2, (half + 1) * TOKENS // 2)
+            nc.sync.dma_start(out=x_sb[:, :, cols], in_=x_tiles[:, :, cols])
+
+        for g in range(M_PASSES):
+            nc.sync.dma_start(out=v_raw[:, g], in_=v_passes[g])
+        load_attention(0)
+        load_attention(1)
+        nc.sync.dma_start(out=wo_raw[:], in_=wo_tiles)
+        load_attention(2)
+        load_x_half(0)
+        load_attention(3)
+        load_x_half(1)
+
+        bo_rows = keep.tile([P, P], BF16)
+        nc.vector.memset(bo_rows[:], 0.0)
+        nc.scalar.dma_start(out=bo_rows[0:O_TILES, :], in_=bo_rows_dram)
+
+        v_grouped = keep.tile([P, M_PASSES, CHANNELS, PACK], BF16, align_bytes=64)
+        v_codes = keep.tile([P, M_PASSES, CHANNELS], U32, align_bytes=64)
+        v_scales = keep.tile([P, M_PASSES, CHANNELS], U8, align_bytes=64)
+
+        def group_v(copy, g, tiles):
+            copy(
+                out=v_grouped[:, g].rearrange("p (t q) j -> p t q j", t=C_TILES)[:, tiles],
+                in_=v_raw[:, g].rearrange("p j (q t) -> p t q j", t=C_TILES)[:, tiles],
+            )
+
+        for g in range(M_PASSES):
+            group_v(nc.vector.tensor_copy, g, slice(0, 2))
+            group_v(nc.scalar.copy, g, slice(2, 3))
+        for g in range(M_PASSES):
+            group_v(nc.vector.tensor_copy, g, slice(3, 4))
+        for cols in (slice(0, CHANNELS // 2), slice(CHANNELS // 2, CHANNELS)):
+            for g in range(M_PASSES):
+                nc.vector.quantize_mx(
+                    out=v_codes[:, g, cols].bitcast(FP8X4),
+                    scales=v_scales[:, g, cols],
+                    in_=v_grouped[:, g, cols, :].rearrange("p c t -> p (c t)"),
+                )
+
+        wo_grouped = keep.tile([P, O_TILES, P, PACK], BF16, align_bytes=64)
+        wo_codes = keep.tile([P, CHANNELS], U32, align_bytes=64)
+        wo_scales = keep.tile([P, CHANNELS], U8, align_bytes=64)
+        bo_column = keep.tile([P, O_TILES], F32)
+
+        def prepare_wo_and_bo():
+            for pair in range(O_TILES // 2):
+                wo_psum = psum_t.tile([P, 2, 2, P], F32, tag="transposed")
+                for k in range(2):
+                    words = wo_raw[:, 2 * pair + k].bitcast(F32)
+                    for u in range(2):
+                        nc.tensor.transpose(wo_psum[:, k, u, :], words[:, u::2], identity_f32[:])
+                copy_out = nc.vector.tensor_copy if pair == 0 else nc.scalar.copy
+                copy_out(
+                    out=wo_grouped[:, 2 * pair : 2 * pair + 2]
+                    .rearrange("p k o t -> p (k o t)")
+                    .bitcast(F32)
+                    .rearrange("p (k o u) -> p k o u", k=2, u=2),
+                    in_=wo_psum[:].rearrange("p k u o -> p k o u"),
+                )
+            bo_psum = psum_t.tile([P, P], BF16, tag="transposed")
+            nc.tensor.transpose(bo_psum[:], bo_rows[:], identity_bf16[:])
+            nc.vector.tensor_copy(out=bo_column[:], in_=bo_psum[:, 0:O_TILES])
+            nc.vector.quantize_mx(
+                out=wo_codes[:].bitcast(FP8X4),
+                scales=wo_scales[:],
+                in_=wo_grouped[:].rearrange("p k o t -> p (k o t)"),
+            )
+
+        a_codes = {}
+        a_scales = {}
+        h_codes = {}
+        h_scales = {}
+
+        def prepare(k):
+            for b in range(k * CHUNK_BLOCKS, (k + 1) * CHUNK_BLOCKS):
+                words = a_raw[b][:].bitcast(F32)
+                transposed = psum_t.tile([P, M_PASSES * 2, P], F32, tag="transposed")
+                for g in range(M_PASSES):
+                    for u in range(2):
+                        nc.tensor.transpose(
+                            transposed[:, 2 * g + u, :],
+                            words[:, 2 * P * g + u : 2 * P * (g + 1) : 2],
+                            identity_f32[:],
+                        )
+                grouped = a_pool.tile(
+                    [P, M_PASSES * P * PACK], BF16, tag="a_grouped", align_bytes=64
+                )
+                nc.scalar.copy(
+                    out=grouped[:].bitcast(F32).rearrange("p (g n u) -> p g n u", g=M_PASSES, u=2),
+                    in_=transposed[:].rearrange("p (g u) n -> p g n u", u=2),
+                )
+                codes = a_pool.tile([P, M_PASSES * P], U32, tag="a_codes", align_bytes=64)
+                scales = a_pool.tile([P, M_PASSES * P], U8, tag="a_scales", align_bytes=64)
+                nc.vector.quantize_mx(out=codes[:].bitcast(FP8X4), scales=scales[:], in_=grouped[:])
+                a_codes[b] = codes
+                a_scales[b] = scales
+
+        def attend(k):
+            grouped = h_pool.tile([P, CHUNK, PACK], BF16, tag="h_grouped", align_bytes=64)
+            codes = h_pool.tile([P, CHUNK], U32, tag="h_codes", align_bytes=64)
+            scales = h_pool.tile([P, CHUNK], U8, tag="h_scales", align_bytes=64)
+            for j in range(CHUNK_BLOCKS):
+                b = k * CHUNK_BLOCKS + j
+                h_psum = psum_h.tile([P, C_TILES, P], F32, tag="h_psum")
+                for t in range(C_TILES):
+                    c_cols = slice(t * P, (t + 1) * P)
+                    for g in range(M_PASSES):
+                        g_cols = slice(g * P, (g + 1) * P)
+                        nc.tensor.matmul_mx(
+                            out=h_psum[:, t, :],
+                            lhsT=v_codes[:, g, c_cols].bitcast(FP8X4),
+                            lhsT_scale=v_scales[:, g, c_cols],
+                            rhs=a_codes[b][:, g_cols].bitcast(FP8X4),
+                            rhs_scale=a_scales[b][:, g_cols],
+                            start=(g == 0),
+                            stop=(g == M_PASSES - 1),
+                        )
+                n_cols = slice(j * P, (j + 1) * P)
+                nc.scalar.copy(out=grouped[:, n_cols, :], in_=h_psum[:].rearrange("p t n -> p n t"))
+                nc.vector.quantize_mx(
+                    out=codes[:, n_cols].bitcast(FP8X4),
+                    scales=scales[:, n_cols],
+                    in_=grouped[:, n_cols, :].rearrange("p n t -> p (n t)"),
+                )
+            h_codes[k] = codes
+            h_scales[k] = scales
+
+        def project(k):
+            n_cols = slice(k * CHUNK, (k + 1) * CHUNK)
+            for bank_tiles in range(0, O_TILES, O_TILES_PER_BANK):
+                p_psum = psum_p.tile([P, O_TILES_PER_BANK, CHUNK], F32, tag="p_psum")
+                for i in range(O_TILES_PER_BANK):
+                    o_tile = bank_tiles + i
+                    o_cols = slice(o_tile * P, (o_tile + 1) * P)
+                    nc.tensor.matmul_mx(
+                        out=p_psum[:, i, :],
+                        lhsT=wo_codes[:, o_cols].bitcast(FP8X4),
+                        lhsT_scale=wo_scales[:, o_cols],
+                        rhs=h_codes[k][:].bitcast(FP8X4),
+                        rhs_scale=h_scales[k][:],
+                        start=True,
+                        stop=True,
+                    )
+                for i in range(O_TILES_PER_BANK):
+                    o_tile = bank_tiles + i
+                    y_sb = y_pool.tile([P, CHUNK], F32, tag="y_sb")
+                    nc.vector.scalar_tensor_tensor(
+                        out=y_sb[:],
+                        in0=p_psum[:, i, :],
+                        scalar=bo_column[:, o_tile : o_tile + 1],
+                        in1=x_sb[:, o_tile, n_cols],
+                        op0=ADD,
+                        op1=ADD,
+                    )
+                    nc.sync.dma_start(out=y_tiles[:, o_tile, n_cols], in_=y_sb[:])
+
+        prepare(0)
+        prepare(1)
+        attend(0)
+        prepare_wo_and_bo()
+        for k in range(CHUNKS):
+            if k + 2 < CHUNKS:
+                prepare(k + 2)
+            project(k)
+            if k + 1 < CHUNKS:
+                attend(k + 1)

@@ -58,8 +58,8 @@ def tile_visionattention_pb_kernel(tc, attention, v, x, Wo, bo, out):
         x_sb = keep.tile([P, O_TILES, TOKENS], BF16)
         a_raw = {}
 
-        def load_attention(k):
-            for b in range(k * CHUNK_BLOCKS, (k + 1) * CHUNK_BLOCKS):
+        def load_attention(blocks):
+            for b in blocks:
                 raw = a_pool.tile([P, TOKENS], BF16, tag="a_raw")
                 nc.sync.dma_start(out=raw[:], in_=attention_blocks[b])
                 a_raw[b] = raw
@@ -68,14 +68,14 @@ def tile_visionattention_pb_kernel(tc, attention, v, x, Wo, bo, out):
             cols = slice(half * TOKENS // 2, (half + 1) * TOKENS // 2)
             nc.sync.dma_start(out=x_sb[:, :, cols], in_=x_tiles[:, :, cols])
 
+        load_attention([0])
         for g in range(M_PASSES):
             nc.sync.dma_start(out=v_raw[:, g], in_=v_passes[g])
-        load_attention(0)
-        load_attention(1)
+        load_attention([1, 2, 3])
         nc.sync.dma_start(out=wo_raw[:], in_=wo_tiles)
-        load_attention(2)
+        load_attention([4, 5])
         load_x_half(0)
-        load_attention(3)
+        load_attention([6, 7])
         load_x_half(1)
 
         bo_rows = keep.tile([P, P], BF16)
@@ -91,19 +91,6 @@ def tile_visionattention_pb_kernel(tc, attention, v, x, Wo, bo, out):
                 out=v_grouped[:, g].rearrange("p (t q) j -> p t q j", t=C_TILES)[:, tiles],
                 in_=v_raw[:, g].rearrange("p j (q t) -> p t q j", t=C_TILES)[:, tiles],
             )
-
-        for g in range(M_PASSES):
-            group_v(nc.vector.tensor_copy, g, slice(0, 2))
-            group_v(nc.scalar.copy, g, slice(2, 3))
-        for g in range(M_PASSES):
-            group_v(nc.vector.tensor_copy, g, slice(3, 4))
-        for cols in (slice(0, CHANNELS // 2), slice(CHANNELS // 2, CHANNELS)):
-            for g in range(M_PASSES):
-                nc.vector.quantize_mx(
-                    out=v_codes[:, g, cols].bitcast(FP8X4),
-                    scales=v_scales[:, g, cols],
-                    in_=v_grouped[:, g, cols, :].rearrange("p c t -> p (c t)"),
-                )
 
         wo_grouped = keep.tile([P, O_TILES, P, PACK], BF16, align_bytes=64)
         wo_codes = keep.tile([P, CHANNELS], U32, align_bytes=64)
@@ -139,8 +126,8 @@ def tile_visionattention_pb_kernel(tc, attention, v, x, Wo, bo, out):
         h_codes = {}
         h_scales = {}
 
-        def prepare(k):
-            for b in range(k * CHUNK_BLOCKS, (k + 1) * CHUNK_BLOCKS):
+        def prepare(blocks):
+            for b in blocks:
                 words = a_raw[b][:].bitcast(F32)
                 transposed = psum_t.tile([P, M_PASSES * 2, P], F32, tag="transposed")
                 for g in range(M_PASSES):
@@ -222,13 +209,28 @@ def tile_visionattention_pb_kernel(tc, attention, v, x, Wo, bo, out):
                     )
                     nc.sync.dma_start(out=y_tiles[:, o_tile, n_cols], in_=y_sb[:])
 
-        prepare(0)
-        prepare(1)
+        prepare([0])
+        for g in range(M_PASSES):
+            group_v(nc.vector.tensor_copy, g, slice(0, 2))
+            group_v(nc.scalar.copy, g, slice(2, 3))
+        for g in range(M_PASSES):
+            group_v(nc.vector.tensor_copy, g, slice(3, 4))
+        for cols in (slice(0, CHANNELS // 2), slice(CHANNELS // 2, CHANNELS)):
+            for g in range(M_PASSES):
+                nc.vector.quantize_mx(
+                    out=v_codes[:, g, cols].bitcast(FP8X4),
+                    scales=v_scales[:, g, cols],
+                    in_=v_grouped[:, g, cols, :].rearrange("p c t -> p (c t)"),
+                )
+        prepare([1, 2, 3])
         attend(0)
         prepare_wo_and_bo()
-        for k in range(CHUNKS):
-            if k + 2 < CHUNKS:
-                prepare(k + 2)
-            project(k)
-            if k + 1 < CHUNKS:
-                attend(k + 1)
+        prepare([4, 5])
+        attend(1)
+        project(0)
+        prepare([6, 7])
+        attend(2)
+        project(1)
+        attend(3)
+        project(2)
+        project(3)

@@ -209,7 +209,27 @@ def tile_visionattention_pb_kernel(tc, attention, v, x, Wo, bo, out):
                     )
                     nc.sync.dma_start(out=y_tiles[:, o_tile, n_cols], in_=y_sb[:])
 
+        busy_psum = psum_p.tile([P, BANK_F32], F32, tag="p_psum")
+        zeros = keep.tile([P, P], F32)
+        nc.vector.memset(zeros[:], 0.0)
+
+        def busy_f32(count):
+            for i in range(count):
+                nc.tensor.matmul(
+                    out=busy_psum[:, 0:P], lhsT=zeros[:], rhs=zeros[:], start=True, stop=True
+                )
+
+        def busy_bf16(rhs):
+            nc.tensor.matmul(
+                out=busy_psum[:], lhsT=identity_bf16[:], rhs=rhs, start=True, stop=True
+            )
+
+        busy_f32(4)
         prepare([0])
+        busy_bf16(a_raw[0][:, 0:BANK_F32])
+        busy_bf16(a_raw[0][:, BANK_F32:TOKENS])
+        busy_bf16(v_raw[:, 0, 0])
+        busy_bf16(v_raw[:, 0, 1])
         for g in range(M_PASSES):
             group_v(nc.vector.tensor_copy, g, slice(0, 2))
             group_v(nc.scalar.copy, g, slice(2, 3))
@@ -222,7 +242,10 @@ def tile_visionattention_pb_kernel(tc, attention, v, x, Wo, bo, out):
                     scales=v_scales[:, g, cols],
                     in_=v_grouped[:, g, cols, :].rearrange("p c t -> p (c t)"),
                 )
-        prepare([1, 2, 3])
+        prepare([1])
+        busy_bf16(a_raw[1][:, 0:BANK_F32])
+        prepare([2, 3])
+        busy_bf16(a_raw[2][:, 0:BANK_F32])
         attend(0)
         prepare_wo_and_bo()
         prepare([4, 5])

@@ -88,8 +88,8 @@ def tile_visionattention_pb_kernel(tc, attention, v, x, Wo, bo, out):
 
         def group_v(copy, g, tiles):
             copy(
-                out=v_grouped[:, g].rearrange("p (t q) j -> p t q j", t=C_TILES)[:, tiles],
-                in_=v_raw[:, g].rearrange("p j (q t) -> p t q j", t=C_TILES)[:, tiles],
+                out=v_grouped[:, g].rearrange("p (t q) j -> p q t j", t=C_TILES)[:, :, tiles],
+                in_=v_raw[:, g].rearrange("p j (q t) -> p q t j", t=C_TILES)[:, :, tiles],
             )
 
         wo_grouped = keep.tile([P, O_TILES, P, PACK], BF16, align_bytes=64)
@@ -127,7 +127,12 @@ def tile_visionattention_pb_kernel(tc, attention, v, x, Wo, bo, out):
         h_scales = {}
 
         def prepare(blocks):
-            for b in blocks:
+            grouped = a_pool.tile(
+                [P, len(blocks), M_PASSES * P * PACK], BF16, tag="a_grouped", align_bytes=64
+            )
+            codes = a_pool.tile([P, len(blocks), M_PASSES * P], U32, tag="a_codes", align_bytes=64)
+            scales = a_pool.tile([P, len(blocks), M_PASSES * P], U8, tag="a_scales", align_bytes=64)
+            for j, b in enumerate(blocks):
                 words = a_raw[b][:].bitcast(F32)
                 transposed = psum_t.tile([P, M_PASSES * 2, P], F32, tag="transposed")
                 for g in range(M_PASSES):
@@ -137,18 +142,17 @@ def tile_visionattention_pb_kernel(tc, attention, v, x, Wo, bo, out):
                             words[:, 2 * P * g + u : 2 * P * (g + 1) : 2],
                             identity_f32[:],
                         )
-                grouped = a_pool.tile(
-                    [P, M_PASSES * P * PACK], BF16, tag="a_grouped", align_bytes=64
-                )
                 nc.scalar.copy(
-                    out=grouped[:].bitcast(F32).rearrange("p (g n u) -> p g n u", g=M_PASSES, u=2),
+                    out=grouped[:, j].bitcast(F32).rearrange("p (g n u) -> p g n u", g=M_PASSES, u=2),
                     in_=transposed[:].rearrange("p (g u) n -> p g n u", u=2),
                 )
-                codes = a_pool.tile([P, M_PASSES * P], U32, tag="a_codes", align_bytes=64)
-                scales = a_pool.tile([P, M_PASSES * P], U8, tag="a_scales", align_bytes=64)
-                nc.vector.quantize_mx(out=codes[:].bitcast(FP8X4), scales=scales[:], in_=grouped[:])
-                a_codes[b] = codes
-                a_scales[b] = scales
+                a_codes[b] = codes[:, j]
+                a_scales[b] = scales[:, j]
+            nc.vector.quantize_mx(
+                out=codes[:].rearrange("p j w -> p (j w)").bitcast(FP8X4),
+                scales=scales[:].rearrange("p j w -> p (j w)"),
+                in_=grouped[:].rearrange("p j w -> p (j w)"),
+            )
 
         def attend(k):
             grouped = h_pool.tile([P, CHUNK, PACK], BF16, tag="h_grouped", align_bytes=64)
@@ -172,11 +176,11 @@ def tile_visionattention_pb_kernel(tc, attention, v, x, Wo, bo, out):
                         )
                 n_cols = slice(j * P, (j + 1) * P)
                 nc.scalar.copy(out=grouped[:, n_cols, :], in_=h_psum[:].rearrange("p t n -> p n t"))
-                nc.vector.quantize_mx(
-                    out=codes[:, n_cols].bitcast(FP8X4),
-                    scales=scales[:, n_cols],
-                    in_=grouped[:, n_cols, :].rearrange("p n t -> p (n t)"),
-                )
+            nc.vector.quantize_mx(
+                out=codes[:].bitcast(FP8X4),
+                scales=scales[:],
+                in_=grouped[:].rearrange("p n t -> p (n t)"),
+            )
             h_codes[k] = codes
             h_scales[k] = scales
 
@@ -230,18 +234,15 @@ def tile_visionattention_pb_kernel(tc, attention, v, x, Wo, bo, out):
         busy_bf16(a_raw[0][:, BANK_F32:TOKENS])
         busy_bf16(v_raw[:, 0, 0])
         busy_bf16(v_raw[:, 0, 1])
+        for g, vector_tiles in ((0, 2), (1, 3)):
+            group_v(nc.vector.tensor_copy, g, slice(0, vector_tiles))
+            group_v(nc.scalar.copy, g, slice(vector_tiles, C_TILES))
         for g in range(M_PASSES):
-            group_v(nc.vector.tensor_copy, g, slice(0, 2))
-            group_v(nc.scalar.copy, g, slice(2, 3))
-        for g in range(M_PASSES):
-            group_v(nc.vector.tensor_copy, g, slice(3, 4))
-        for cols in (slice(0, CHANNELS // 2), slice(CHANNELS // 2, CHANNELS)):
-            for g in range(M_PASSES):
-                nc.vector.quantize_mx(
-                    out=v_codes[:, g, cols].bitcast(FP8X4),
-                    scales=v_scales[:, g, cols],
-                    in_=v_grouped[:, g, cols, :].rearrange("p c t -> p (c t)"),
-                )
+            nc.vector.quantize_mx(
+                out=v_codes[:, g].bitcast(FP8X4),
+                scales=v_scales[:, g],
+                in_=v_grouped[:, g].rearrange("p c t -> p (c t)"),
+            )
         prepare([1])
         busy_bf16(a_raw[1][:, 0:BANK_F32])
         prepare([2, 3])

@@ -249,8 +249,8 @@ def tile_visionattention_pb_kernel(tc, attention, v, x, Wo, bo, out):
         busy_bf16(a_raw[2][:, 0:BANK_F32])
         attend(0)
         prepare_wo_and_bo()
-        prepare([4, 5])
         attend(1)
+        prepare([4, 5])
         project(0)
         prepare([6, 7])
         attend(2)

@@ -44,8 +44,8 @@ def tile_visionattention_pb_kernel(tc, attention, v, x, Wo, bo, out):
         a_pool = ctx.enter_context(tc.tile_pool(name="a", bufs=BLOCKS))
         h_pool = ctx.enter_context(tc.tile_pool(name="h", bufs=2))
         y_pool = ctx.enter_context(tc.tile_pool(name="y", bufs=2 * O_TILES))
-        psum_t = ctx.enter_context(tc.psum_pool(name="psum_t", bufs=4))
-        psum_h = ctx.enter_context(tc.psum_pool(name="psum_h", bufs=2))
+        psum_t = ctx.enter_context(tc.psum_pool(name="psum_t", bufs=3))
+        psum_h = ctx.enter_context(tc.psum_pool(name="psum_h", bufs=3))
         psum_p = ctx.enter_context(tc.psum_pool(name="psum_p", bufs=2))
 
         identity_f32 = keep.tile([P, P], F32)
@@ -158,6 +158,14 @@ def tile_visionattention_pb_kernel(tc, attention, v, x, Wo, bo, out):
             grouped = h_pool.tile([P, CHUNK, PACK], BF16, tag="h_grouped", align_bytes=64)
             codes = h_pool.tile([P, CHUNK], U32, tag="h_codes", align_bytes=64)
             scales = h_pool.tile([P, CHUNK], U8, tag="h_scales", align_bytes=64)
+
+            def quantize_h(n_cols):
+                nc.vector.quantize_mx(
+                    out=codes[:, n_cols].bitcast(FP8X4),
+                    scales=scales[:, n_cols],
+                    in_=grouped[:, n_cols, :].rearrange("p n t -> p (n t)"),
+                )
+
             for j in range(CHUNK_BLOCKS):
                 b = k * CHUNK_BLOCKS + j
                 h_psum = psum_h.tile([P, C_TILES, P], F32, tag="h_psum")
@@ -176,11 +184,10 @@ def tile_visionattention_pb_kernel(tc, attention, v, x, Wo, bo, out):
                         )
                 n_cols = slice(j * P, (j + 1) * P)
                 nc.scalar.copy(out=grouped[:, n_cols, :], in_=h_psum[:].rearrange("p t n -> p n t"))
-            nc.vector.quantize_mx(
-                out=codes[:].bitcast(FP8X4),
-                scales=scales[:],
-                in_=grouped[:].rearrange("p n t -> p (n t)"),
-            )
+                if k == CHUNKS - 1:
+                    quantize_h(n_cols)
+            if k < CHUNKS - 1:
+                quantize_h(slice(0, CHUNK))
             h_codes[k] = codes
             h_scales[k] = scales
 
@@ -212,6 +219,37 @@ def tile_visionattention_pb_kernel(tc, attention, v, x, Wo, bo, out):
                         op1=ADD,
                     )
                     nc.sync.dma_start(out=y_tiles[:, o_tile, n_cols], in_=y_sb[:])
+
+        def project_block(b):
+            k, j = divmod(b, CHUNK_BLOCKS)
+            n_cols = slice(b * P, (b + 1) * P)
+            h_cols = slice(j * P, (j + 1) * P)
+            p_psum = psum_t.tile([P, O_TILES, P], F32, tag="transposed")
+            for o_tile in range(O_TILES):
+                o_cols = slice(o_tile * P, (o_tile + 1) * P)
+                nc.tensor.matmul_mx(
+                    out=p_psum[:, o_tile, :],
+                    lhsT=wo_codes[:, o_cols].bitcast(FP8X4),
+                    lhsT_scale=wo_scales[:, o_cols],
+                    rhs=h_codes[k][:, h_cols].bitcast(FP8X4),
+                    rhs_scale=h_scales[k][:, h_cols],
+                    start=True,
+                    stop=True,
+                )
+            for half in range(2):
+                tiles = slice(half * O_TILES // 2, (half + 1) * O_TILES // 2)
+                y_sb = y_pool.tile([P, O_TILES // 2, P], F32, tag="y_sb")
+                for i in range(O_TILES // 2):
+                    o_tile = half * O_TILES // 2 + i
+                    nc.vector.scalar_tensor_tensor(
+                        out=y_sb[:, i, :],
+                        in0=p_psum[:, o_tile, :],
+                        scalar=bo_column[:, o_tile : o_tile + 1],
+                        in1=x_sb[:, o_tile, n_cols],
+                        op0=ADD,
+                        op1=ADD,
+                    )
+                nc.sync.dma_start(out=y_tiles[:, tiles, n_cols], in_=y_sb[:])
 
         busy_psum = psum_p.tile([P, BANK_F32], F32, tag="p_psum")
         zeros = keep.tile([P, P], F32)
@@ -250,11 +288,14 @@ def tile_visionattention_pb_kernel(tc, attention, v, x, Wo, bo, out):
         attend(0)
         prepare_wo_and_bo()
         attend(1)
-        prepare([4, 5])
+        prepare([4])
+        prepare([5])
         project(0)
-        prepare([6, 7])
+        prepare([6])
+        prepare([7])
         attend(2)
         project(1)
         attend(3)
         project(2)
-        project(3)
+        project_block(6)
+        project_block(7)

@@ -272,6 +272,8 @@ def tile_visionattention_pb_kernel(tc, attention, v, x, Wo, bo, out):
         busy_bf16(a_raw[0][:, BANK_F32:TOKENS])
         busy_bf16(v_raw[:, 0, 0])
         busy_bf16(v_raw[:, 0, 1])
+        busy_bf16(v_raw[:, 1, 0])
+        busy_bf16(v_raw[:, 1, 1])
         for g, vector_tiles in ((0, 2), (1, 3)):
             group_v(nc.vector.tensor_copy, g, slice(0, vector_tiles))
             group_v(nc.scalar.copy, g, slice(vector_tiles, C_TILES))

@@ -284,9 +284,7 @@ def tile_visionattention_pb_kernel(tc, attention, v, x, Wo, bo, out):
                 in_=v_grouped[:, g].rearrange("p c t -> p (c t)"),
             )
         prepare([1])
-        busy_bf16(a_raw[1][:, 0:BANK_F32])
         prepare([2, 3])
-        busy_bf16(a_raw[2][:, 0:BANK_F32])
         attend(0)
         prepare_wo_and_bo()
         attend(1)

@@ -42,7 +42,6 @@ def tile_visionattention_pb_kernel(tc, attention, v, x, Wo, bo, out):
     with ExitStack() as ctx:
         keep = ctx.enter_context(tc.tile_pool(name="keep", bufs=1))
         a_pool = ctx.enter_context(tc.tile_pool(name="a", bufs=BLOCKS))
-        h_pool = ctx.enter_context(tc.tile_pool(name="h", bufs=2))
         y_pool = ctx.enter_context(tc.tile_pool(name="y", bufs=2 * O_TILES))
         psum_t = ctx.enter_context(tc.psum_pool(name="psum_t", bufs=3))
         psum_h = ctx.enter_context(tc.psum_pool(name="psum_h", bufs=3))
@@ -73,9 +72,8 @@ def tile_visionattention_pb_kernel(tc, attention, v, x, Wo, bo, out):
             nc.sync.dma_start(out=v_raw[:, g], in_=v_passes[g])
         load_attention([1, 2, 3])
         nc.sync.dma_start(out=wo_raw[:], in_=wo_tiles)
-        load_attention([4, 5])
+        load_attention([4, 5, 6, 7])
         load_x_half(0)
-        load_attention([6, 7])
         load_x_half(1)
 
         bo_rows = keep.tile([P, P], BF16)
@@ -92,18 +90,26 @@ def tile_visionattention_pb_kernel(tc, attention, v, x, Wo, bo, out):
                 in_=v_raw[:, g].rearrange("p j (q t) -> p q t j", t=C_TILES)[:, :, tiles],
             )
 
+        wo_sorted = keep.tile([P, O_TILES, 2, P], F32)
         wo_grouped = keep.tile([P, O_TILES, P, PACK], BF16, align_bytes=64)
         wo_codes = keep.tile([P, CHANNELS], U32, align_bytes=64)
         wo_scales = keep.tile([P, CHANNELS], U8, align_bytes=64)
         bo_column = keep.tile([P, O_TILES], F32)
 
-        def prepare_wo_and_bo():
+        def sort_wo():
+            nc.vector.tensor_copy(
+                out=wo_sorted[:],
+                in_=wo_raw[:].bitcast(F32).rearrange("p k (w u) -> p k u w", u=2),
+            )
+
+        def transpose_wo():
             for pair in range(O_TILES // 2):
                 wo_psum = psum_t.tile([P, 2, 2, P], F32, tag="transposed")
                 for k in range(2):
-                    words = wo_raw[:, 2 * pair + k].bitcast(F32)
                     for u in range(2):
-                        nc.tensor.transpose(wo_psum[:, k, u, :], words[:, u::2], identity_f32[:])
+                        nc.tensor.transpose(
+                            wo_psum[:, k, u, :], wo_sorted[:, 2 * pair + k, u, :], identity_f32[:]
+                        )
                 copy_out = nc.vector.tensor_copy if pair == 0 else nc.scalar.copy
                 copy_out(
                     out=wo_grouped[:, 2 * pair : 2 * pair + 2]
@@ -112,143 +118,134 @@ def tile_visionattention_pb_kernel(tc, attention, v, x, Wo, bo, out):
                     .rearrange("p (k o u) -> p k o u", k=2, u=2),
                     in_=wo_psum[:].rearrange("p k u o -> p k o u"),
                 )
+
+        def finish_wo_and_bo():
             bo_psum = psum_t.tile([P, P], BF16, tag="transposed")
             nc.tensor.transpose(bo_psum[:], bo_rows[:], identity_bf16[:])
-            nc.vector.tensor_copy(out=bo_column[:], in_=bo_psum[:, 0:O_TILES])
             nc.vector.quantize_mx(
                 out=wo_codes[:].bitcast(FP8X4),
                 scales=wo_scales[:],
                 in_=wo_grouped[:].rearrange("p k o t -> p (k o t)"),
             )
+            nc.vector.tensor_copy(out=bo_column[:], in_=bo_psum[:, 0:O_TILES])
 
+        a_sorted = {}
+        a_grouped = {}
         a_codes = {}
         a_scales = {}
-        h_codes = {}
-        h_scales = {}
 
-        def prepare(blocks):
+        def a_words(b):
+            return a_raw[b][:].bitcast(F32).rearrange("p (g w u) -> p g u w", g=M_PASSES, u=2)
+
+        def sort_a(b):
+            a_sorted[b] = a_pool.tile([P, M_PASSES, 2, P], F32, tag="a_sorted", name="a_sorted")
+            nc.vector.tensor_copy(out=a_sorted[b][:], in_=a_words(b))
+
+        def transpose_a(*blocks):
             grouped = a_pool.tile(
                 [P, len(blocks), M_PASSES * P * PACK], BF16, tag="a_grouped", align_bytes=64
             )
-            codes = a_pool.tile([P, len(blocks), M_PASSES * P], U32, tag="a_codes", align_bytes=64)
-            scales = a_pool.tile([P, len(blocks), M_PASSES * P], U8, tag="a_scales", align_bytes=64)
+            a_grouped[blocks] = grouped
             for j, b in enumerate(blocks):
-                words = a_raw[b][:].bitcast(F32)
+                words = a_sorted[b] if b in a_sorted else a_words(b)
                 transposed = psum_t.tile([P, M_PASSES * 2, P], F32, tag="transposed")
                 for g in range(M_PASSES):
                     for u in range(2):
                         nc.tensor.transpose(
-                            transposed[:, 2 * g + u, :],
-                            words[:, 2 * P * g + u : 2 * P * (g + 1) : 2],
-                            identity_f32[:],
+                            transposed[:, 2 * g + u, :], words[:, g, u, :], identity_f32[:]
                         )
                 nc.scalar.copy(
                     out=grouped[:, j].bitcast(F32).rearrange("p (g n u) -> p g n u", g=M_PASSES, u=2),
                     in_=transposed[:].rearrange("p (g u) n -> p g n u", u=2),
                 )
-                a_codes[b] = codes[:, j]
-                a_scales[b] = scales[:, j]
+
+        def quantize_a(*blocks):
+            codes = a_pool.tile([P, len(blocks), M_PASSES * P], U32, tag="a_codes", align_bytes=64)
+            scales = a_pool.tile([P, len(blocks), M_PASSES * P], U8, tag="a_scales", align_bytes=64)
             nc.vector.quantize_mx(
                 out=codes[:].rearrange("p j w -> p (j w)").bitcast(FP8X4),
                 scales=scales[:].rearrange("p j w -> p (j w)"),
-                in_=grouped[:].rearrange("p j w -> p (j w)"),
+                in_=a_grouped[blocks][:].rearrange("p j w -> p (j w)"),
+            )
+            for j, b in enumerate(blocks):
+                a_codes[b] = codes[:, j]
+                a_scales[b] = scales[:, j]
+
+        h_grouped = keep.tile([P, TOKENS, PACK], BF16, align_bytes=64)
+        h_codes = keep.tile([P, TOKENS], U32, align_bytes=64)
+        h_scales = keep.tile([P, TOKENS], U8, align_bytes=64)
+
+        def attend(b):
+            h_psum = psum_h.tile([P, C_TILES, P], F32, tag="h_psum")
+            for t in range(C_TILES):
+                c_cols = slice(t * P, (t + 1) * P)
+                for g in range(M_PASSES):
+                    g_cols = slice(g * P, (g + 1) * P)
+                    nc.tensor.matmul_mx(
+                        out=h_psum[:, t, :],
+                        lhsT=v_codes[:, g, c_cols].bitcast(FP8X4),
+                        lhsT_scale=v_scales[:, g, c_cols],
+                        rhs=a_codes[b][:, g_cols].bitcast(FP8X4),
+                        rhs_scale=a_scales[b][:, g_cols],
+                        start=(g == 0),
+                        stop=(g == M_PASSES - 1),
+                    )
+            nc.scalar.copy(
+                out=h_grouped[:, b * P : (b + 1) * P, :], in_=h_psum[:].rearrange("p t n -> p n t")
             )
 
-        def attend(k):
-            grouped = h_pool.tile([P, CHUNK, PACK], BF16, tag="h_grouped", align_bytes=64)
-            codes = h_pool.tile([P, CHUNK], U32, tag="h_codes", align_bytes=64)
-            scales = h_pool.tile([P, CHUNK], U8, tag="h_scales", align_bytes=64)
+        def quantize_h(first, count):
+            n_cols = slice(first * P, (first + count) * P)
+            nc.vector.quantize_mx(
+                out=h_codes[:, n_cols].bitcast(FP8X4),
+                scales=h_scales[:, n_cols],
+                in_=h_grouped[:, n_cols, :].rearrange("p n t -> p (n t)"),
+            )
 
-            def quantize_h(n_cols):
-                nc.vector.quantize_mx(
-                    out=codes[:, n_cols].bitcast(FP8X4),
-                    scales=scales[:, n_cols],
-                    in_=grouped[:, n_cols, :].rearrange("p n t -> p (n t)"),
-                )
+        def multiply_wo(out, o_tile, n_cols):
+            o_cols = slice(o_tile * P, (o_tile + 1) * P)
+            nc.tensor.matmul_mx(
+                out=out,
+                lhsT=wo_codes[:, o_cols].bitcast(FP8X4),
+                lhsT_scale=wo_scales[:, o_cols],
+                rhs=h_codes[:, n_cols].bitcast(FP8X4),
+                rhs_scale=h_scales[:, n_cols],
+                start=True,
+                stop=True,
+            )
 
-            for j in range(CHUNK_BLOCKS):
-                b = k * CHUNK_BLOCKS + j
-                h_psum = psum_h.tile([P, C_TILES, P], F32, tag="h_psum")
-                for t in range(C_TILES):
-                    c_cols = slice(t * P, (t + 1) * P)
-                    for g in range(M_PASSES):
-                        g_cols = slice(g * P, (g + 1) * P)
-                        nc.tensor.matmul_mx(
-                            out=h_psum[:, t, :],
-                            lhsT=v_codes[:, g, c_cols].bitcast(FP8X4),
-                            lhsT_scale=v_scales[:, g, c_cols],
-                            rhs=a_codes[b][:, g_cols].bitcast(FP8X4),
-                            rhs_scale=a_scales[b][:, g_cols],
-                            start=(g == 0),
-                            stop=(g == M_PASSES - 1),
-                        )
-                n_cols = slice(j * P, (j + 1) * P)
-                nc.scalar.copy(out=grouped[:, n_cols, :], in_=h_psum[:].rearrange("p t n -> p n t"))
-                if k == CHUNKS - 1:
-                    quantize_h(n_cols)
-            if k < CHUNKS - 1:
-                quantize_h(slice(0, CHUNK))
-            h_codes[k] = codes
-            h_scales[k] = scales
+        def add_x_and_bo(out, p, o_tile, n_cols):
+            nc.vector.scalar_tensor_tensor(
+                out=out,
+                in0=p,
+                scalar=bo_column[:, o_tile : o_tile + 1],
+                in1=x_sb[:, o_tile, n_cols],
+                op0=ADD,
+                op1=ADD,
+            )
 
-        def project(k):
+        def project_half(k, half):
             n_cols = slice(k * CHUNK, (k + 1) * CHUNK)
-            for bank_tiles in range(0, O_TILES, O_TILES_PER_BANK):
-                p_psum = psum_p.tile([P, O_TILES_PER_BANK, CHUNK], F32, tag="p_psum")
-                for i in range(O_TILES_PER_BANK):
-                    o_tile = bank_tiles + i
-                    o_cols = slice(o_tile * P, (o_tile + 1) * P)
-                    nc.tensor.matmul_mx(
-                        out=p_psum[:, i, :],
-                        lhsT=wo_codes[:, o_cols].bitcast(FP8X4),
-                        lhsT_scale=wo_scales[:, o_cols],
-                        rhs=h_codes[k][:].bitcast(FP8X4),
-                        rhs_scale=h_scales[k][:],
-                        start=True,
-                        stop=True,
-                    )
-                for i in range(O_TILES_PER_BANK):
-                    o_tile = bank_tiles + i
-                    y_sb = y_pool.tile([P, CHUNK], F32, tag="y_sb")
-                    nc.vector.scalar_tensor_tensor(
-                        out=y_sb[:],
-                        in0=p_psum[:, i, :],
-                        scalar=bo_column[:, o_tile : o_tile + 1],
-                        in1=x_sb[:, o_tile, n_cols],
-                        op0=ADD,
-                        op1=ADD,
-                    )
-                    nc.sync.dma_start(out=y_tiles[:, o_tile, n_cols], in_=y_sb[:])
+            p_psum = psum_p.tile([P, O_TILES_PER_BANK, CHUNK], F32, tag="p_psum")
+            for i in range(O_TILES_PER_BANK):
+                multiply_wo(p_psum[:, i, :], half * O_TILES_PER_BANK + i, n_cols)
+            for i in range(O_TILES_PER_BANK):
+                o_tile = half * O_TILES_PER_BANK + i
+                y_sb = y_pool.tile([P, CHUNK], F32, tag="y_sb")
+                add_x_and_bo(y_sb[:], p_psum[:, i, :], o_tile, n_cols)
+                nc.sync.dma_start(out=y_tiles[:, o_tile, n_cols], in_=y_sb[:])
 
         def project_block(b):
-            k, j = divmod(b, CHUNK_BLOCKS)
             n_cols = slice(b * P, (b + 1) * P)
-            h_cols = slice(j * P, (j + 1) * P)
             p_psum = psum_t.tile([P, O_TILES, P], F32, tag="transposed")
             for o_tile in range(O_TILES):
-                o_cols = slice(o_tile * P, (o_tile + 1) * P)
-                nc.tensor.matmul_mx(
-                    out=p_psum[:, o_tile, :],
-                    lhsT=wo_codes[:, o_cols].bitcast(FP8X4),
-                    lhsT_scale=wo_scales[:, o_cols],
-                    rhs=h_codes[k][:, h_cols].bitcast(FP8X4),
-                    rhs_scale=h_scales[k][:, h_cols],
-                    start=True,
-                    stop=True,
-                )
+                multiply_wo(p_psum[:, o_tile, :], o_tile, n_cols)
             for half in range(2):
                 tiles = slice(half * O_TILES // 2, (half + 1) * O_TILES // 2)
                 y_sb = y_pool.tile([P, O_TILES // 2, P], F32, tag="y_sb")
                 for i in range(O_TILES // 2):
                     o_tile = half * O_TILES // 2 + i
-                    nc.vector.scalar_tensor_tensor(
-                        out=y_sb[:, i, :],
-                        in0=p_psum[:, o_tile, :],
-                        scalar=bo_column[:, o_tile : o_tile + 1],
-                        in1=x_sb[:, o_tile, n_cols],
-                        op0=ADD,
-                        op1=ADD,
-                    )
+                    add_x_and_bo(y_sb[:, i, :], p_psum[:, o_tile, :], o_tile, n_cols)
                 nc.sync.dma_start(out=y_tiles[:, tiles, n_cols], in_=y_sb[:])
 
         busy_psum = psum_p.tile([P, BANK_F32], F32, tag="p_psum")
@@ -267,35 +264,59 @@ def tile_visionattention_pb_kernel(tc, attention, v, x, Wo, bo, out):
             )
 
         busy_f32(4)
-        prepare([0])
-        busy_bf16(a_raw[0][:, 0:BANK_F32])
-        busy_bf16(a_raw[0][:, BANK_F32:TOKENS])
-        busy_bf16(v_raw[:, 0, 0])
-        busy_bf16(v_raw[:, 0, 1])
-        busy_bf16(v_raw[:, 1, 0])
-        busy_bf16(v_raw[:, 1, 1])
-        for g, vector_tiles in ((0, 2), (1, 3)):
-            group_v(nc.vector.tensor_copy, g, slice(0, vector_tiles))
-            group_v(nc.scalar.copy, g, slice(vector_tiles, C_TILES))
-        for g in range(M_PASSES):
-            nc.vector.quantize_mx(
-                out=v_codes[:, g].bitcast(FP8X4),
-                scales=v_scales[:, g],
-                in_=v_grouped[:, g].rearrange("p c t -> p (c t)"),
-            )
-        prepare([1])
-        prepare([2, 3])
-        attend(0)
-        prepare_wo_and_bo()
-        attend(1)
-        prepare([4])
-        prepare([5])
-        project(0)
-        prepare([6])
-        prepare([7])
-        attend(2)
-        project(1)
-        attend(3)
-        project(2)
-        project_block(6)
-        project_block(7)
+        with tc.manual_schedule(engines={mybir.EngineType.DVE}):
+            for g, vector_tiles in ((0, 2), (1, 3)):
+                group_v(nc.vector.tensor_copy, g, slice(0, vector_tiles))
+                group_v(nc.scalar.copy, g, slice(vector_tiles, C_TILES))
+            for g in range(M_PASSES):
+                nc.vector.quantize_mx(
+                    out=v_codes[:, g].bitcast(FP8X4),
+                    scales=v_scales[:, g],
+                    in_=v_grouped[:, g].rearrange("p c t -> p (c t)"),
+                )
+            transpose_a(0)
+            quantize_a(0)
+            busy_bf16(a_raw[0][:, 0:BANK_F32])
+            busy_bf16(a_raw[0][:, BANK_F32:TOKENS])
+            busy_bf16(v_raw[:, 0, 0])
+            busy_bf16(v_raw[:, 0, 1])
+            busy_bf16(v_raw[:, 1, 0])
+            busy_bf16(v_raw[:, 1, 1])
+            transpose_a(1)
+            quantize_a(1)
+            sort_wo()
+            transpose_a(2, 3)
+            quantize_a(2, 3)
+            attend(0)
+            attend(1)
+            transpose_wo()
+            quantize_h(0, 2)
+            finish_wo_and_bo()
+            sort_a(6)
+            sort_a(7)
+            attend(2)
+            attend(3)
+            quantize_h(2, 2)
+            transpose_a(4)
+            quantize_a(4)
+            transpose_a(5)
+            project_half(0, 0)
+            quantize_a(5)
+            project_half(0, 1)
+            transpose_a(6)
+            quantize_a(6)
+            transpose_a(7)
+            quantize_a(7)
+            attend(4)
+            attend(5)
+            project_half(1, 0)
+            quantize_h(4, 2)
+            project_half(1, 1)
+            attend(6)
+            quantize_h(6, 1)
+            attend(7)
+            project_half(2, 0)
+            quantize_h(7, 1)
+            project_half(2, 1)
+            project_block(6)
+            project_block(7)

@@ -224,9 +224,9 @@ def tile_visionattention_pb_kernel(tc, attention, v, x, Wo, bo, out):
                 op1=ADD,
             )
 
-        def project_half(k, half):
+        def project_half(k, half, pool=psum_p, tag="p_psum"):
             n_cols = slice(k * CHUNK, (k + 1) * CHUNK)
-            p_psum = psum_p.tile([P, O_TILES_PER_BANK, CHUNK], F32, tag="p_psum")
+            p_psum = pool.tile([P, O_TILES_PER_BANK, CHUNK], F32, tag=tag)
             for i in range(O_TILES_PER_BANK):
                 multiply_wo(p_psum[:, i, :], half * O_TILES_PER_BANK + i, n_cols)
             for i in range(O_TILES_PER_BANK):
@@ -289,6 +289,8 @@ def tile_visionattention_pb_kernel(tc, attention, v, x, Wo, bo, out):
             quantize_a(2, 3)
             attend(0)
             attend(1)
+            sort_a(4)
+            sort_a(5)
             transpose_wo()
             quantize_h(0, 2)
             finish_wo_and_bo()
@@ -315,8 +317,8 @@ def tile_visionattention_pb_kernel(tc, attention, v, x, Wo, bo, out):
             attend(6)
             quantize_h(6, 1)
             attend(7)
-            project_half(2, 0)
+            project_half(2, 0, psum_t, "transposed")
             quantize_h(7, 1)
-            project_half(2, 1)
+            project_half(2, 1, psum_t, "transposed")
             project_block(6)
             project_block(7)

@@ -43,8 +43,8 @@ def tile_visionattention_pb_kernel(tc, attention, v, x, Wo, bo, out):
         keep = ctx.enter_context(tc.tile_pool(name="keep", bufs=1))
         a_pool = ctx.enter_context(tc.tile_pool(name="a", bufs=BLOCKS))
         y_pool = ctx.enter_context(tc.tile_pool(name="y", bufs=2 * O_TILES))
-        psum_t = ctx.enter_context(tc.psum_pool(name="psum_t", bufs=3))
-        psum_h = ctx.enter_context(tc.psum_pool(name="psum_h", bufs=3))
+        psum_t = ctx.enter_context(tc.psum_pool(name="psum_t", bufs=4))
+        psum_h = ctx.enter_context(tc.psum_pool(name="psum_h", bufs=2))
         psum_p = ctx.enter_context(tc.psum_pool(name="psum_p", bufs=2))
 
         identity_f32 = keep.tile([P, P], F32)
@@ -284,26 +284,28 @@ def tile_visionattention_pb_kernel(tc, attention, v, x, Wo, bo, out):
             busy_bf16(v_raw[:, 1, 1])
             transpose_a(1)
             quantize_a(1)
+            busy_bf16(a_raw[1][:, 0:BANK_F32])
             sort_wo()
             transpose_a(2, 3)
             quantize_a(2, 3)
+            busy_bf16(a_raw[2][:, 0:BANK_F32])
             attend(0)
             attend(1)
             sort_a(4)
             sort_a(5)
             transpose_wo()
+            transpose_a(4)
+            transpose_a(5)
             quantize_h(0, 2)
             finish_wo_and_bo()
+            quantize_a(4)
             sort_a(6)
+            quantize_a(5)
             sort_a(7)
             attend(2)
             attend(3)
             quantize_h(2, 2)
-            transpose_a(4)
-            quantize_a(4)
-            transpose_a(5)
             project_half(0, 0)
-            quantize_a(5)
             project_half(0, 1)
             transpose_a(6)
             quantize_a(6)

@@ -34,10 +34,10 @@ def tile_visionattention_pb_kernel(tc, attention, v, x, Wo, bo, out):
 
     attention_blocks = attention.rearrange("b (k p) m -> (b k) p m", p=P)
     v_passes = v.rearrange("b (g q j) c -> (b g) q j c", g=M_PASSES, j=PACK)
-    wo_tiles = Wo.rearrange("(t p) c -> p t c", p=P)
-    bo_rows_dram = bo.rearrange("(t p) -> t p", p=P)
-    x_tiles = x.rearrange("b (t p) i j -> p (b t) (i j)", p=P)
-    y_tiles = out.rearrange("b (t p) i j -> p (b t) (i j)", p=P)
+    wo_tiles = Wo.rearrange("(p t) c -> p t c", t=O_TILES)
+    bo_tiles = bo.rearrange("(p t) -> p t", t=O_TILES)
+    x_tiles = x.rearrange("b (p t) i j -> (b p) t (i j)", t=O_TILES)
+    y_tiles = out.rearrange("b (p t) i j -> (b p) t (i j)", t=O_TILES)
 
     with ExitStack() as ctx:
         keep = ctx.enter_context(tc.tile_pool(name="keep", bufs=1))
@@ -63,22 +63,16 @@ def tile_visionattention_pb_kernel(tc, attention, v, x, Wo, bo, out):
                 nc.sync.dma_start(out=raw[:], in_=attention_blocks[b])
                 a_raw[b] = raw
 
-        def load_x_half(half):
-            cols = slice(half * TOKENS // 2, (half + 1) * TOKENS // 2)
-            nc.sync.dma_start(out=x_sb[:, :, cols], in_=x_tiles[:, :, cols])
-
         load_attention([0])
         for g in range(M_PASSES):
             nc.sync.dma_start(out=v_raw[:, g], in_=v_passes[g])
         load_attention([1, 2, 3])
         nc.sync.dma_start(out=wo_raw[:], in_=wo_tiles)
         load_attention([4, 5, 6, 7])
-        load_x_half(0)
-        load_x_half(1)
+        nc.sync.dma_start(out=x_sb[:], in_=x_tiles)
 
-        bo_rows = keep.tile([P, P], BF16)
-        nc.vector.memset(bo_rows[:], 0.0)
-        nc.scalar.dma_start(out=bo_rows[0:O_TILES, :], in_=bo_rows_dram)
+        bo_sb = keep.tile([P, O_TILES], BF16)
+        nc.scalar.dma_start(out=bo_sb[:], in_=bo_tiles)
 
         v_grouped = keep.tile([P, M_PASSES, CHANNELS, PACK], BF16, align_bytes=64)
         v_codes = keep.tile([P, M_PASSES, CHANNELS], U32, align_bytes=64)
@@ -94,7 +88,6 @@ def tile_visionattention_pb_kernel(tc, attention, v, x, Wo, bo, out):
         wo_grouped = keep.tile([P, O_TILES, P, PACK], BF16, align_bytes=64)
         wo_codes = keep.tile([P, CHANNELS], U32, align_bytes=64)
         wo_scales = keep.tile([P, CHANNELS], U8, align_bytes=64)
-        bo_column = keep.tile([P, O_TILES], F32)
 
         def sort_wo():
             nc.vector.tensor_copy(
@@ -119,15 +112,12 @@ def tile_visionattention_pb_kernel(tc, attention, v, x, Wo, bo, out):
                     in_=wo_psum[:].rearrange("p k u o -> p k o u"),
                 )
 
-        def finish_wo_and_bo():
-            bo_psum = psum_t.tile([P, P], BF16, tag="transposed")
-            nc.tensor.transpose(bo_psum[:], bo_rows[:], identity_bf16[:])
+        def quantize_wo():
             nc.vector.quantize_mx(
                 out=wo_codes[:].bitcast(FP8X4),
                 scales=wo_scales[:],
                 in_=wo_grouped[:].rearrange("p k o t -> p (k o t)"),
             )
-            nc.vector.tensor_copy(out=bo_column[:], in_=bo_psum[:, 0:O_TILES])
 
         a_sorted = {}
         a_grouped = {}
@@ -218,7 +208,7 @@ def tile_visionattention_pb_kernel(tc, attention, v, x, Wo, bo, out):
             nc.vector.scalar_tensor_tensor(
                 out=out,
                 in0=p,
-                scalar=bo_column[:, o_tile : o_tile + 1],
+                scalar=bo_sb[:, o_tile : o_tile + 1],
                 in1=x_sb[:, o_tile, n_cols],
                 op0=ADD,
                 op1=ADD,
@@ -297,7 +287,7 @@ def tile_visionattention_pb_kernel(tc, attention, v, x, Wo, bo, out):
             transpose_a(4)
             transpose_a(5)
             quantize_h(0, 2)
-            finish_wo_and_bo()
+            quantize_wo()
             quantize_a(4)
             sort_a(6)
             quantize_a(5)

@@ -225,19 +225,6 @@ def tile_visionattention_pb_kernel(tc, attention, v, x, Wo, bo, out):
                 add_x_and_bo(y_sb[:], p_psum[:, i, :], o_tile, n_cols)
                 nc.sync.dma_start(out=y_tiles[:, o_tile, n_cols], in_=y_sb[:])
 
-        def project_block(b):
-            n_cols = slice(b * P, (b + 1) * P)
-            p_psum = psum_t.tile([P, O_TILES, P], F32, tag="transposed")
-            for o_tile in range(O_TILES):
-                multiply_wo(p_psum[:, o_tile, :], o_tile, n_cols)
-            for half in range(2):
-                tiles = slice(half * O_TILES // 2, (half + 1) * O_TILES // 2)
-                y_sb = y_pool.tile([P, O_TILES // 2, P], F32, tag="y_sb")
-                for i in range(O_TILES // 2):
-                    o_tile = half * O_TILES // 2 + i
-                    add_x_and_bo(y_sb[:, i, :], p_psum[:, o_tile, :], o_tile, n_cols)
-                nc.sync.dma_start(out=y_tiles[:, tiles, n_cols], in_=y_sb[:])
-
         busy_psum = psum_p.tile([P, BANK_F32], F32, tag="p_psum")
         zeros = keep.tile([P, P], F32)
         nc.vector.memset(zeros[:], 0.0)
@@ -307,10 +294,9 @@ def tile_visionattention_pb_kernel(tc, attention, v, x, Wo, bo, out):
             quantize_h(4, 2)
             project_half(1, 1)
             attend(6)
-            quantize_h(6, 1)
             attend(7)
             project_half(2, 0, psum_t, "transposed")
-            quantize_h(7, 1)
+            quantize_h(6, 2)
             project_half(2, 1, psum_t, "transposed")
-            project_block(6)
-            project_block(7)
+            project_half(3, 0, psum_t, "transposed")
+            project_half(3, 1, psum_t, "transposed")

@@ -72,7 +72,7 @@ def tile_visionattention_pb_kernel(tc, attention, v, x, Wo, bo, out):
         nc.sync.dma_start(out=x_sb[:], in_=x_tiles)
 
         bo_sb = keep.tile([P, O_TILES], BF16)
-        nc.scalar.dma_start(out=bo_sb[:], in_=bo_tiles)
+        nc.sync.dma_start(out=bo_sb[:], in_=bo_tiles)
 
         v_grouped = keep.tile([P, M_PASSES, CHANNELS, PACK], BF16, align_bytes=64)
         v_codes = keep.tile([P, M_PASSES, CHANNELS], U32, align_bytes=64)
@@ -242,6 +242,7 @@ def tile_visionattention_pb_kernel(tc, attention, v, x, Wo, bo, out):
 
         busy_f32(4)
         with tc.manual_schedule(engines={mybir.EngineType.DVE}):
+            transpose_a(0)
             for g, vector_tiles in ((0, 2), (1, 3)):
                 group_v(nc.vector.tensor_copy, g, slice(0, vector_tiles))
                 group_v(nc.scalar.copy, g, slice(vector_tiles, C_TILES))
@@ -251,7 +252,6 @@ def tile_visionattention_pb_kernel(tc, attention, v, x, Wo, bo, out):
                     scales=v_scales[:, g],
                     in_=v_grouped[:, g].rearrange("p c t -> p (c t)"),
                 )
-            transpose_a(0)
             quantize_a(0)
             busy_bf16(a_raw[0][:, 0:BANK_F32])
             busy_bf16(a_raw[0][:, BANK_F32:TOKENS])

@@ -259,13 +259,13 @@ def tile_visionattention_pb_kernel(tc, attention, v, x, Wo, bo, out):
             busy_bf16(v_raw[:, 0, 1])
             busy_bf16(v_raw[:, 1, 0])
             busy_bf16(v_raw[:, 1, 1])
+            busy_bf16(v_raw[:, 1, 2])
             transpose_a(1)
             quantize_a(1)
             busy_bf16(a_raw[1][:, 0:BANK_F32])
             sort_wo()
             transpose_a(2, 3)
             quantize_a(2, 3)
-            busy_bf16(a_raw[2][:, 0:BANK_F32])
             attend(0)
             attend(1)
             sort_a(4)

@@ -69,10 +69,12 @@ def tile_visionattention_pb_kernel(tc, attention, v, x, Wo, bo, out):
         load_attention([1, 2, 3])
         nc.sync.dma_start(out=wo_raw[:], in_=wo_tiles)
         load_attention([4, 5, 6, 7])
-        nc.sync.dma_start(out=x_sb[:], in_=x_tiles)
 
         bo_sb = keep.tile([P, O_TILES], BF16)
         nc.sync.dma_start(out=bo_sb[:], in_=bo_tiles)
+        for half in range(2):
+            n_cols = slice(half * TOKENS // 2, (half + 1) * TOKENS // 2)
+            nc.sync.dma_start(out=x_sb[:, :, n_cols], in_=x_tiles[:, :, n_cols])
 
         v_grouped = keep.tile([P, M_PASSES, CHANNELS, PACK], BF16, align_bytes=64)
         v_codes = keep.tile([P, M_PASSES, CHANNELS], U32, align_bytes=64)

@@ -279,12 +279,12 @@ def tile_visionattention_pb_kernel(tc, attention, v, x, Wo, bo, out):
             quantize_wo()
             quantize_a(4)
             sort_a(6)
-            quantize_a(5)
             sort_a(7)
             attend(2)
             attend(3)
-            quantize_h(2, 2)
             project_half(0, 0)
+            quantize_a(5)
+            quantize_h(2, 2)
             project_half(0, 1)
             transpose_a(6)
             quantize_a(6)

from contextlib import ExitStack

import concourse.mybir as mybir
from concourse.masks import make_identity

F32 = mybir.dt.float32
BF16 = mybir.dt.bfloat16
U32 = mybir.dt.uint32
U8 = mybir.dt.uint8
FP8X4 = mybir.dt.float8_e4m3fn_x4
ADD = mybir.AluOpType.add

P = 128
PACK = 4
K_PASS = P * PACK

TOKENS = 1024
CHANNELS = 512
M_PASSES = TOKENS // K_PASS
C_TILES = CHANNELS // P
O_TILES = CHANNELS // P
BLOCKS = TOKENS // P
CHUNK_BLOCKS = 2
CHUNK = CHUNK_BLOCKS * P
CHUNKS = BLOCKS // CHUNK_BLOCKS
BANK_F32 = 512
O_TILES_PER_BANK = BANK_F32 // CHUNK

FLOPS = 2 * TOKENS * TOKENS * CHANNELS + 2 * CHANNELS * CHANNELS * TOKENS


def tile_visionattention_pb_kernel(tc, attention, v, x, Wo, bo, out):
    nc = tc.nc

    attention_blocks = attention.rearrange("b (k p) m -> (b k) p m", p=P)
    v_passes = v.rearrange("b (g q j) c -> (b g) q j c", g=M_PASSES, j=PACK)
    wo_tiles = Wo.rearrange("(p t) c -> p t c", t=O_TILES)
    bo_tiles = bo.rearrange("(p t) -> p t", t=O_TILES)
    x_tiles = x.rearrange("b (p t) i j -> (b p) t (i j)", t=O_TILES)
    y_tiles = out.rearrange("b (p t) i j -> (b p) t (i j)", t=O_TILES)

    with ExitStack() as ctx:
        keep = ctx.enter_context(tc.tile_pool(name="keep", bufs=1))
        a_pool = ctx.enter_context(tc.tile_pool(name="a", bufs=BLOCKS))
        y_pool = ctx.enter_context(tc.tile_pool(name="y", bufs=2 * O_TILES))
        psum_t = ctx.enter_context(tc.psum_pool(name="psum_t", bufs=4))
        psum_h = ctx.enter_context(tc.psum_pool(name="psum_h", bufs=2))
        psum_p = ctx.enter_context(tc.psum_pool(name="psum_p", bufs=2))

        identity_f32 = keep.tile([P, P], F32)
        make_identity(nc, identity_f32[:])
        identity_bf16 = keep.tile([P, P], BF16)
        make_identity(nc, identity_bf16[:])

        v_raw = keep.tile([P, M_PASSES, PACK, CHANNELS], BF16)
        wo_raw = keep.tile([P, O_TILES, CHANNELS], BF16)
        x_sb = keep.tile([P, O_TILES, TOKENS], BF16)
        a_raw = {}

        def load_attention(blocks):
            for b in blocks:
                raw = a_pool.tile([P, TOKENS], BF16, tag="a_raw")
                nc.sync.dma_start(out=raw[:], in_=attention_blocks[b])
                a_raw[b] = raw

        load_attention([0])
        for g in range(M_PASSES):
            nc.sync.dma_start(out=v_raw[:, g], in_=v_passes[g])
        load_attention([1, 2, 3])
        nc.sync.dma_start(out=wo_raw[:], in_=wo_tiles)
        load_attention([4, 5, 6, 7])

        bo_sb = keep.tile([P, O_TILES], BF16)
        nc.sync.dma_start(out=bo_sb[:], in_=bo_tiles)
        for half in range(2):
            n_cols = slice(half * TOKENS // 2, (half + 1) * TOKENS // 2)
            nc.sync.dma_start(out=x_sb[:, :, n_cols], in_=x_tiles[:, :, n_cols])

        v_grouped = keep.tile([P, M_PASSES, CHANNELS, PACK], BF16, align_bytes=64)
        v_codes = keep.tile([P, M_PASSES, CHANNELS], U32, align_bytes=64)
        v_scales = keep.tile([P, M_PASSES, CHANNELS], U8, align_bytes=64)

        def group_v(copy, g, tiles):
            copy(
                out=v_grouped[:, g].rearrange("p (t q) j -> p q t j", t=C_TILES)[:, :, tiles],
                in_=v_raw[:, g].rearrange("p j (q t) -> p q t j", t=C_TILES)[:, :, tiles],
            )

        wo_sorted = keep.tile([P, O_TILES, 2, P], F32)
        wo_grouped = keep.tile([P, O_TILES, P, PACK], BF16, align_bytes=64)
        wo_codes = keep.tile([P, CHANNELS], U32, align_bytes=64)
        wo_scales = keep.tile([P, CHANNELS], U8, align_bytes=64)

        def sort_wo():
            nc.vector.tensor_copy(
                out=wo_sorted[:],
                in_=wo_raw[:].bitcast(F32).rearrange("p k (w u) -> p k u w", u=2),
            )

        def transpose_wo():
            for pair in range(O_TILES // 2):
                wo_psum = psum_t.tile([P, 2, 2, P], F32, tag="transposed")
                for k in range(2):
                    for u in range(2):
                        nc.tensor.transpose(
                            wo_psum[:, k, u, :], wo_sorted[:, 2 * pair + k, u, :], identity_f32[:]
                        )
                copy_out = nc.vector.tensor_copy if pair == 0 else nc.scalar.copy
                copy_out(
                    out=wo_grouped[:, 2 * pair : 2 * pair + 2]
                    .rearrange("p k o t -> p (k o t)")
                    .bitcast(F32)
                    .rearrange("p (k o u) -> p k o u", k=2, u=2),
                    in_=wo_psum[:].rearrange("p k u o -> p k o u"),
                )

        def quantize_wo():
            nc.vector.quantize_mx(
                out=wo_codes[:].bitcast(FP8X4),
                scales=wo_scales[:],
                in_=wo_grouped[:].rearrange("p k o t -> p (k o t)"),
            )

        a_sorted = {}
        a_grouped = {}
        a_codes = {}
        a_scales = {}

        def a_words(b):
            return a_raw[b][:].bitcast(F32).rearrange("p (g w u) -> p g u w", g=M_PASSES, u=2)

        def sort_a(b):
            a_sorted[b] = a_pool.tile([P, M_PASSES, 2, P], F32, tag="a_sorted", name="a_sorted")
            nc.vector.tensor_copy(out=a_sorted[b][:], in_=a_words(b))

        def transpose_a(*blocks):
            grouped = a_pool.tile(
                [P, len(blocks), M_PASSES * P * PACK], BF16, tag="a_grouped", align_bytes=64
            )
            a_grouped[blocks] = grouped
            for j, b in enumerate(blocks):
                words = a_sorted[b] if b in a_sorted else a_words(b)
                transposed = psum_t.tile([P, M_PASSES * 2, P], F32, tag="transposed")
                for g in range(M_PASSES):
                    for u in range(2):
                        nc.tensor.transpose(
                            transposed[:, 2 * g + u, :], words[:, g, u, :], identity_f32[:]
                        )
                nc.scalar.copy(
                    out=grouped[:, j].bitcast(F32).rearrange("p (g n u) -> p g n u", g=M_PASSES, u=2),
                    in_=transposed[:].rearrange("p (g u) n -> p g n u", u=2),
                )

        def quantize_a(*blocks):
            codes = a_pool.tile([P, len(blocks), M_PASSES * P], U32, tag="a_codes", align_bytes=64)
            scales = a_pool.tile([P, len(blocks), M_PASSES * P], U8, tag="a_scales", align_bytes=64)
            nc.vector.quantize_mx(
                out=codes[:].rearrange("p j w -> p (j w)").bitcast(FP8X4),
                scales=scales[:].rearrange("p j w -> p (j w)"),
                in_=a_grouped[blocks][:].rearrange("p j w -> p (j w)"),
            )
            for j, b in enumerate(blocks):
                a_codes[b] = codes[:, j]
                a_scales[b] = scales[:, j]

        h_grouped = keep.tile([P, TOKENS, PACK], BF16, align_bytes=64)
        h_codes = keep.tile([P, TOKENS], U32, align_bytes=64)
        h_scales = keep.tile([P, TOKENS], U8, align_bytes=64)

        def attend(b):
            h_psum = psum_h.tile([P, C_TILES, P], F32, tag="h_psum")
            for t in range(C_TILES):
                c_cols = slice(t * P, (t + 1) * P)
                for g in range(M_PASSES):
                    g_cols = slice(g * P, (g + 1) * P)
                    nc.tensor.matmul_mx(
                        out=h_psum[:, t, :],
                        lhsT=v_codes[:, g, c_cols].bitcast(FP8X4),
                        lhsT_scale=v_scales[:, g, c_cols],
                        rhs=a_codes[b][:, g_cols].bitcast(FP8X4),
                        rhs_scale=a_scales[b][:, g_cols],
                        start=(g == 0),
                        stop=(g == M_PASSES - 1),
                    )
            nc.scalar.copy(
                out=h_grouped[:, b * P : (b + 1) * P, :], in_=h_psum[:].rearrange("p t n -> p n t")
            )

        def quantize_h(first, count):
            n_cols = slice(first * P, (first + count) * P)
            nc.vector.quantize_mx(
                out=h_codes[:, n_cols].bitcast(FP8X4),
                scales=h_scales[:, n_cols],
                in_=h_grouped[:, n_cols, :].rearrange("p n t -> p (n t)"),
            )

        def multiply_wo(out, o_tile, n_cols):
            o_cols = slice(o_tile * P, (o_tile + 1) * P)
            nc.tensor.matmul_mx(
                out=out,
                lhsT=wo_codes[:, o_cols].bitcast(FP8X4),
                lhsT_scale=wo_scales[:, o_cols],
                rhs=h_codes[:, n_cols].bitcast(FP8X4),
                rhs_scale=h_scales[:, n_cols],
                start=True,
                stop=True,
            )

        def add_x_and_bo(out, p, o_tile, n_cols):
            nc.vector.scalar_tensor_tensor(
                out=out,
                in0=p,
                scalar=bo_sb[:, o_tile : o_tile + 1],
                in1=x_sb[:, o_tile, n_cols],
                op0=ADD,
                op1=ADD,
            )

        def project_half(k, half, pool=psum_p, tag="p_psum"):
            n_cols = slice(k * CHUNK, (k + 1) * CHUNK)
            p_psum = pool.tile([P, O_TILES_PER_BANK, CHUNK], F32, tag=tag)
            for i in range(O_TILES_PER_BANK):
                multiply_wo(p_psum[:, i, :], half * O_TILES_PER_BANK + i, n_cols)
            for i in range(O_TILES_PER_BANK):
                o_tile = half * O_TILES_PER_BANK + i
                y_sb = y_pool.tile([P, CHUNK], F32, tag="y_sb")
                add_x_and_bo(y_sb[:], p_psum[:, i, :], o_tile, n_cols)
                nc.sync.dma_start(out=y_tiles[:, o_tile, n_cols], in_=y_sb[:])

        busy_psum = psum_p.tile([P, BANK_F32], F32, tag="p_psum")
        zeros = keep.tile([P, P], F32)
        nc.vector.memset(zeros[:], 0.0)

        def busy_f32(count):
            for i in range(count):
                nc.tensor.matmul(
                    out=busy_psum[:, 0:P], lhsT=zeros[:], rhs=zeros[:], start=True, stop=True
                )

        def busy_bf16(rhs):
            nc.tensor.matmul(
                out=busy_psum[:], lhsT=identity_bf16[:], rhs=rhs, start=True, stop=True
            )

        busy_f32(4)
        with tc.manual_schedule(engines={mybir.EngineType.DVE}):
            transpose_a(0)
            for g, vector_tiles in ((0, 2), (1, 3)):
                group_v(nc.vector.tensor_copy, g, slice(0, vector_tiles))
                group_v(nc.scalar.copy, g, slice(vector_tiles, C_TILES))
            for g in range(M_PASSES):
                nc.vector.quantize_mx(
                    out=v_codes[:, g].bitcast(FP8X4),
                    scales=v_scales[:, g],
                    in_=v_grouped[:, g].rearrange("p c t -> p (c t)"),
                )
            quantize_a(0)
            busy_bf16(a_raw[0][:, 0:BANK_F32])
            busy_bf16(a_raw[0][:, BANK_F32:TOKENS])
            busy_bf16(v_raw[:, 0, 0])
            busy_bf16(v_raw[:, 0, 1])
            busy_bf16(v_raw[:, 1, 0])
            busy_bf16(v_raw[:, 1, 1])
            busy_bf16(v_raw[:, 1, 2])
            transpose_a(1)
            quantize_a(1)
            busy_bf16(a_raw[1][:, 0:BANK_F32])
            sort_wo()
            transpose_a(2, 3)
            quantize_a(2, 3)
            attend(0)
            attend(1)
            sort_a(4)
            sort_a(5)
            transpose_wo()
            transpose_a(4)
            transpose_a(5)
            quantize_h(0, 2)
            quantize_wo()
            quantize_a(4)
            sort_a(6)
            sort_a(7)
            attend(2)
            attend(3)
            project_half(0, 0)
            quantize_a(5)
            quantize_h(2, 2)
            project_half(0, 1)
            transpose_a(6)
            quantize_a(6)
            transpose_a(7)
            quantize_a(7)
            attend(4)
            attend(5)
            project_half(1, 0)
            quantize_h(4, 2)
            project_half(1, 1)
            attend(6)
            attend(7)
            project_half(2, 0, psum_t, "transposed")
            quantize_h(6, 2)
            project_half(2, 1, psum_t, "transposed")
            project_half(3, 0, psum_t, "transposed")
            project_half(3, 1, psum_t, "transposed")
